import numpy as np
import ml_dtypes

BF16 = ml_dtypes.bfloat16


def bf(x):
    return np.asarray(x, np.float32).astype(BF16)


def f32(x):
    return np.asarray(x, np.float32)


def f64(x):
    return np.asarray(x).astype(np.float64)


def striped(idx):
    return np.tile(idx.reshape(-1, 16).T, (8, 1))


C, S, N = 128, 4096, 512


def unit_columns(v):
    return v / np.sqrt(np.sum(v * v, axis=0, keepdims=True))


def setup_inputs():
    mu = np.random.standard_normal((C, 1))
    base = f32(unit_columns(np.random.standard_normal((C, S)) + mu))
    dirs = f32(np.random.standard_normal((C, N)) + mu)
    return {"base": base, "dirs": dirs, "offs": striped(np.random.permutation(S)[:N])}


def reference(base, dirs, offs):
    idx = offs[:16].T.reshape(-1)
    d = f64(dirs)
    r = 1.0 / np.sqrt(np.sum(d * d, axis=0, keepdims=True))
    out = f64(base).copy()
    out[:, idx] = d * r
    return out

@@ -1,0 +1,37 @@
+import concourse.mybir as mybir
+
+C, S, N = 128, 4096, 512
+F32, BF16, U16 = mybir.dt.float32, mybir.dt.bfloat16, mybir.dt.uint16
+MULT = mybir.AluOpType.mult
+SQRT = mybir.ActivationFunctionType.Sqrt
+
+FLOPS = 3 * C * N
+
+
+def tile_directionalignmentloss_kernel(tc, base, dirs, offs, out):
+    nc = tc.nc
+    with (
+        tc.tile_pool(name="held", bufs=1) as held,
+        tc.psum_pool(name="psum", bufs=1) as psum,
+    ):
+        offsets = held.tile([C, N // 16], U16, name="offsets")
+        nc.sync.dma_start(offsets[:], offs)
+        samples = held.tile([C, N], F32, name="samples")
+        nc.scalar.dma_start(samples[:], dirs)
+        window = held.tile([C, S], F32, name="window")
+        nc.sync.dma_start(window[:], base)
+
+        ones = held.tile([C, C], BF16, name="ones")
+        nc.gpsimd.memset(ones[:], 1.0)
+        squares = held.tile([C, N], BF16, name="squares")
+        nc.vector.tensor_tensor(squares[:], samples[:], samples[:], MULT)
+        sums = psum.tile([C, N], F32, name="sums")
+        nc.tensor.matmul(sums[:], ones[:], squares[:], start=True, stop=True)
+
+        lengths = held.tile([C, N], F32, name="lengths")
+        nc.scalar.activation(lengths[:], sums[:], SQRT)
+        inverse = held.tile([C, N], F32, name="inverse")
+        nc.vector.reciprocal(inverse[:], lengths[:])
+
+        nc.vector.tensor_tensor(window[:].indirect(offsets[:]), samples[:], inverse[:], MULT)
+        nc.sync.dma_start(out, window[:])

@@ -1,6 +1,8 @@
 import concourse.mybir as mybir
+from concourse.masks import make_identity
 
 C, S, N = 128, 4096, 512
+BLOCKS = N // C
 F32, BF16, U16 = mybir.dt.float32, mybir.dt.bfloat16, mybir.dt.uint16
 MULT = mybir.AluOpType.mult
 SQRT = mybir.ActivationFunctionType.Sqrt
@@ -21,17 +23,27 @@ def tile_directionalignmentloss_kernel(tc, base, dirs, offs, out):
         window = held.tile([C, S], F32, name="window")
         nc.sync.dma_start(window[:], base)
 
-        ones = held.tile([C, C], BF16, name="ones")
+        ones = held.tile([C, 1], BF16, name="ones")
         nc.gpsimd.memset(ones[:], 1.0)
+        identity = held.tile([C, C], F32, name="identity")
+        make_identity(nc, identity[:])
+
         squares = held.tile([C, N], BF16, name="squares")
         nc.vector.tensor_tensor(squares[:], samples[:], samples[:], MULT)
-        sums = psum.tile([C, N], F32, name="sums")
-        nc.tensor.matmul(sums[:], ones[:], squares[:], start=True, stop=True)
+        sums = psum.tile([C, BLOCKS], F32, name="sums")
+        for b in range(BLOCKS):
+            nc.tensor.matmul(sums[:, b : b + 1], squares[:, b * C : (b + 1) * C], ones[:], start=True, stop=True)
 
-        lengths = held.tile([C, N], F32, name="lengths")
+        lengths = held.tile([C, BLOCKS], F32, name="lengths")
         nc.scalar.activation(lengths[:], sums[:], SQRT)
-        inverse = held.tile([C, N], F32, name="inverse")
+        inverse = held.tile([C, BLOCKS], F32, name="inverse")
         nc.vector.reciprocal(inverse[:], lengths[:])
 
-        nc.vector.tensor_tensor(window[:].indirect(offsets[:]), samples[:], inverse[:], MULT)
+        spread = psum.tile([C, N], F32, name="spread")
+        for b in range(BLOCKS):
+            nc.tensor.transpose(spread[:, b * C : (b + 1) * C], inverse[:, b : b + 1].to_broadcast([C, C]), identity[:])
+        scales = held.tile([C, N], F32, name="scales")
+        nc.vector.tensor_copy(scales[:], spread[:])
+
+        nc.vector.tensor_tensor(window[:].indirect(offsets[:]), samples[:], scales[:], MULT)
         nc.sync.dma_start(out, window[:])

@@ -2,7 +2,9 @@ import concourse.mybir as mybir
 from concourse.masks import make_identity
 
 C, S, N = 128, 4096, 512
-BLOCKS = N // C
+HALVES = 2
+H = N // HALVES
+BLOCKS = H // C
 F32, BF16, U16 = mybir.dt.float32, mybir.dt.bfloat16, mybir.dt.uint16
 MULT = mybir.AluOpType.mult
 SQRT = mybir.ActivationFunctionType.Sqrt
@@ -16,10 +18,10 @@ def tile_directionalignmentloss_kernel(tc, base, dirs, offs, out):
         tc.tile_pool(name="held", bufs=1) as held,
         tc.psum_pool(name="psum", bufs=1) as psum,
     ):
+        samples = held.tile([C, N], F32, name="samples")
+        nc.sync.dma_start(samples[:], dirs)
         offsets = held.tile([C, N // 16], U16, name="offsets")
         nc.sync.dma_start(offsets[:], offs)
-        samples = held.tile([C, N], F32, name="samples")
-        nc.scalar.dma_start(samples[:], dirs)
         window = held.tile([C, S], F32, name="window")
         nc.sync.dma_start(window[:], base)
 
@@ -28,22 +30,30 @@ def tile_directionalignmentloss_kernel(tc, base, dirs, offs, out):
         identity = held.tile([C, C], F32, name="identity")
         make_identity(nc, identity[:])
 
-        squares = held.tile([C, N], BF16, name="squares")
-        nc.vector.tensor_tensor(squares[:], samples[:], samples[:], MULT)
-        sums = psum.tile([C, BLOCKS], F32, name="sums")
-        for b in range(BLOCKS):
-            nc.tensor.matmul(sums[:, b : b + 1], squares[:, b * C : (b + 1) * C], ones[:], start=True, stop=True)
-
-        lengths = held.tile([C, BLOCKS], F32, name="lengths")
-        nc.scalar.activation(lengths[:], sums[:], SQRT)
-        inverse = held.tile([C, BLOCKS], F32, name="inverse")
-        nc.vector.reciprocal(inverse[:], lengths[:])
-
-        spread = psum.tile([C, N], F32, name="spread")
-        for b in range(BLOCKS):
-            nc.tensor.transpose(spread[:, b * C : (b + 1) * C], inverse[:, b : b + 1].to_broadcast([C, C]), identity[:])
+        halves = range(HALVES)
+        squares = [held.tile([C, H], BF16, name=f"squares{h}") for h in halves]
+        sums = [psum.tile([C, BLOCKS], F32, name=f"sums{h}") for h in halves]
+        lengths = [held.tile([C, BLOCKS], F32, name=f"lengths{h}") for h in halves]
+        inverse = [held.tile([C, BLOCKS], F32, name=f"inverse{h}") for h in halves]
+        spread = [psum.tile([C, H], F32, name=f"spread{h}") for h in halves]
         scales = held.tile([C, N], F32, name="scales")
-        nc.vector.tensor_copy(scales[:], spread[:])
+
+        for h in halves:
+            nc.vector.tensor_tensor(squares[h][:], samples[:, h * H : (h + 1) * H], samples[:, h * H : (h + 1) * H], MULT)
+        for h in halves:
+            for b in range(BLOCKS):
+                nc.tensor.matmul(sums[h][:, b : b + 1], squares[h][:, b * C : (b + 1) * C], ones[:], start=True, stop=True)
+
+        for h in halves:
+            nc.scalar.activation(lengths[h][:], sums[h][:], SQRT)
+        for h in halves:
+            nc.vector.reciprocal(inverse[h][:], lengths[h][:])
+
+        for h in halves:
+            for b in range(BLOCKS):
+                nc.tensor.transpose(spread[h][:, b * C : (b + 1) * C], inverse[h][:, b : b + 1].to_broadcast([C, C]), identity[:])
+        nc.scalar.copy(scales[:, 0:H], spread[0][:])
+        nc.vector.tensor_copy(scales[:, H:N], spread[1][:])
 
         nc.vector.tensor_tensor(window[:].indirect(offsets[:]), samples[:], scales[:], MULT)
         nc.sync.dma_start(out, window[:])

@@ -33,7 +33,6 @@ def tile_directionalignmentloss_kernel(tc, base, dirs, offs, out):
         halves = range(HALVES)
         squares = [held.tile([C, H], BF16, name=f"squares{h}") for h in halves]
         sums = [psum.tile([C, BLOCKS], F32, name=f"sums{h}") for h in halves]
-        lengths = [held.tile([C, BLOCKS], F32, name=f"lengths{h}") for h in halves]
         inverse = [held.tile([C, BLOCKS], F32, name=f"inverse{h}") for h in halves]
         spread = [psum.tile([C, H], F32, name=f"spread{h}") for h in halves]
         scales = held.tile([C, N], F32, name="scales")
@@ -45,15 +44,14 @@ def tile_directionalignmentloss_kernel(tc, base, dirs, offs, out):
                 nc.tensor.matmul(sums[h][:, b : b + 1], squares[h][:, b * C : (b + 1) * C], ones[:], start=True, stop=True)
 
         for h in halves:
-            nc.scalar.activation(lengths[h][:], sums[h][:], SQRT)
-        for h in halves:
-            nc.vector.reciprocal(inverse[h][:], lengths[h][:])
+            nc.vector.reciprocal(inverse[h][:], sums[h][:])
 
         for h in halves:
             for b in range(BLOCKS):
                 nc.tensor.transpose(spread[h][:, b * C : (b + 1) * C], inverse[h][:, b : b + 1].to_broadcast([C, C]), identity[:])
-        nc.scalar.copy(scales[:, 0:H], spread[0][:])
-        nc.vector.tensor_copy(scales[:, H:N], spread[1][:])
+
+        for h in halves:
+            nc.scalar.activation(scales[:, h * H : (h + 1) * H], spread[h][:], SQRT)
 
         nc.vector.tensor_tensor(window[:].indirect(offsets[:]), samples[:], scales[:], MULT)
         nc.sync.dma_start(out, window[:])

@@ -2,6 +2,7 @@ import concourse.mybir as mybir
 from concourse.masks import make_identity
 
 C, S, N = 128, 4096, 512
+WINDOWS = 2
 HALVES = 2
 H = N // HALVES
 BLOCKS = H // C
@@ -22,8 +23,9 @@ def tile_directionalignmentloss_kernel(tc, base, dirs, offs, out):
         nc.sync.dma_start(samples[:], dirs)
         offsets = held.tile([C, N // 16], U16, name="offsets")
         nc.sync.dma_start(offsets[:], offs)
-        window = held.tile([C, S], F32, name="window")
-        nc.sync.dma_start(window[:], base)
+        windows = [held.tile([C, S], F32, name=f"window{k}") for k in range(WINDOWS)]
+        for k in range(WINDOWS):
+            nc.sync.dma_start(windows[k][k:C:WINDOWS, :], base[k:C:WINDOWS, :])
 
         ones = held.tile([C, 1], BF16, name="ones")
         nc.gpsimd.memset(ones[:], 1.0)
@@ -53,5 +55,6 @@ def tile_directionalignmentloss_kernel(tc, base, dirs, offs, out):
         for h in halves:
             nc.scalar.activation(scales[:, h * H : (h + 1) * H], spread[h][:], SQRT)
 
-        nc.vector.tensor_tensor(window[:].indirect(offsets[:]), samples[:], scales[:], MULT)
-        nc.sync.dma_start(out, window[:])
+        for k in range(WINDOWS):
+            nc.vector.tensor_tensor(windows[k][:].indirect(offsets[:]), samples[:], scales[:], MULT)
+            nc.sync.dma_start(out[k:C:WINDOWS, :], windows[k][k:C:WINDOWS, :])

@@ -1,14 +1,12 @@
 import concourse.mybir as mybir
-from concourse.masks import make_identity
 
 C, S, N = 128, 4096, 512
 WINDOWS = 2
 HALVES = 2
 H = N // HALVES
-BLOCKS = H // C
 F32, BF16, U16 = mybir.dt.float32, mybir.dt.bfloat16, mybir.dt.uint16
 MULT = mybir.AluOpType.mult
-SQRT = mybir.ActivationFunctionType.Sqrt
+RSQRT = mybir.ActivationFunctionType.Abs_reciprocal_sqrt
 
 FLOPS = 3 * C * N
 
@@ -27,33 +25,20 @@ def tile_directionalignmentloss_kernel(tc, base, dirs, offs, out):
         for k in range(WINDOWS):
             nc.sync.dma_start(windows[k][k:C:WINDOWS, :], base[k:C:WINDOWS, :])
 
-        ones = held.tile([C, 1], BF16, name="ones")
+        ones = held.tile([C, C], BF16, name="ones")
         nc.gpsimd.memset(ones[:], 1.0)
-        identity = held.tile([C, C], F32, name="identity")
-        make_identity(nc, identity[:])
 
         halves = range(HALVES)
         squares = [held.tile([C, H], BF16, name=f"squares{h}") for h in halves]
-        sums = [psum.tile([C, BLOCKS], F32, name=f"sums{h}") for h in halves]
-        inverse = [held.tile([C, BLOCKS], F32, name=f"inverse{h}") for h in halves]
-        spread = [psum.tile([C, H], F32, name=f"spread{h}") for h in halves]
+        sums = [psum.tile([C, H], F32, name=f"sums{h}") for h in halves]
         scales = held.tile([C, N], F32, name="scales")
 
         for h in halves:
             nc.vector.tensor_tensor(squares[h][:], samples[:, h * H : (h + 1) * H], samples[:, h * H : (h + 1) * H], MULT)
         for h in halves:
-            for b in range(BLOCKS):
-                nc.tensor.matmul(sums[h][:, b : b + 1], squares[h][:, b * C : (b + 1) * C], ones[:], start=True, stop=True)
-
+            nc.tensor.matmul(sums[h][:], ones[:], squares[h][:], start=True, stop=True)
         for h in halves:
-            nc.vector.reciprocal(inverse[h][:], sums[h][:])
-
-        for h in halves:
-            for b in range(BLOCKS):
-                nc.tensor.transpose(spread[h][:, b * C : (b + 1) * C], inverse[h][:, b : b + 1].to_broadcast([C, C]), identity[:])
-
-        for h in halves:
-            nc.scalar.activation(scales[:, h * H : (h + 1) * H], spread[h][:], SQRT)
+            nc.scalar.activation(scales[:, h * H : (h + 1) * H], sums[h][:], RSQRT)
 
         for k in range(WINDOWS):
             nc.vector.tensor_tensor(windows[k][:].indirect(offsets[:]), samples[:], scales[:], MULT)

@@ -19,11 +19,11 @@ def tile_directionalignmentloss_kernel(tc, base, dirs, offs, out):
     ):
         samples = held.tile([C, N], F32, name="samples")
         nc.sync.dma_start(samples[:], dirs)
-        offsets = held.tile([C, N // 16], U16, name="offsets")
-        nc.sync.dma_start(offsets[:], offs)
         windows = [held.tile([C, S], F32, name=f"window{k}") for k in range(WINDOWS)]
-        for k in range(WINDOWS):
-            nc.sync.dma_start(windows[k][k:C:WINDOWS, :], base[k:C:WINDOWS, :])
+        offsets = held.tile([C, N // 16], U16, name="offsets")
+        nc.sync.dma_start(windows[0][0:C:WINDOWS, :], base[0:C:WINDOWS, :])
+        nc.sync.dma_start(offsets[:], offs)
+        nc.sync.dma_start(windows[1][1:C:WINDOWS, :], base[1:C:WINDOWS, :])
 
         ones = held.tile([C, C], BF16, name="ones")
         nc.gpsimd.memset(ones[:], 1.0)

@@ -15,30 +15,34 @@ def tile_directionalignmentloss_kernel(tc, base, dirs, offs, out):
     nc = tc.nc
     with (
         tc.tile_pool(name="held", bufs=1) as held,
+        tc.tile_pool(name="lent", bufs=1) as lent,
         tc.psum_pool(name="psum", bufs=1) as psum,
     ):
         samples = held.tile([C, N], F32, name="samples")
         nc.sync.dma_start(samples[:], dirs)
-        windows = [held.tile([C, S], F32, name=f"window{k}") for k in range(WINDOWS)]
+        window0 = held.tile([C, S], F32, name="window0")
         offsets = held.tile([C, N // 16], U16, name="offsets")
-        nc.sync.dma_start(windows[0][0:C:WINDOWS, :], base[0:C:WINDOWS, :])
         nc.sync.dma_start(offsets[:], offs)
-        nc.sync.dma_start(windows[1][1:C:WINDOWS, :], base[1:C:WINDOWS, :])
+        nc.sync.dma_start(window0[0:C:WINDOWS, :], base[0:C:WINDOWS, :])
 
         ones = held.tile([C, C], BF16, name="ones")
         nc.gpsimd.memset(ones[:], 1.0)
 
         halves = range(HALVES)
-        squares = [held.tile([C, H], BF16, name=f"squares{h}") for h in halves]
+        squares = lent.tile([C, HALVES, H], BF16, name="squares", tag="shared")
         sums = [psum.tile([C, H], F32, name=f"sums{h}") for h in halves]
         scales = held.tile([C, N], F32, name="scales")
 
         for h in halves:
-            nc.vector.tensor_tensor(squares[h][:], samples[:, h * H : (h + 1) * H], samples[:, h * H : (h + 1) * H], MULT)
+            nc.vector.tensor_tensor(squares[:, h, :], samples[:, h * H : (h + 1) * H], samples[:, h * H : (h + 1) * H], MULT)
         for h in halves:
-            nc.tensor.matmul(sums[h][:], ones[:], squares[h][:], start=True, stop=True)
+            nc.tensor.matmul(sums[h][:], ones[:], squares[:, h, :], start=True, stop=True)
         for h in halves:
             nc.scalar.activation(scales[:, h * H : (h + 1) * H], sums[h][:], RSQRT)
+
+        window1 = lent.tile([C, S], F32, name="window1", tag="shared")
+        nc.sync.dma_start(window1[1:C:WINDOWS, :], base[1:C:WINDOWS, :])
+        windows = [window0, window1]
 
         for k in range(WINDOWS):
             nc.vector.tensor_tensor(windows[k][:].indirect(offsets[:]), samples[:], scales[:], MULT)

@@ -26,7 +26,7 @@ def tile_directionalignmentloss_kernel(tc, base, dirs, offs, out):
         nc.sync.dma_start(window0[0:C:WINDOWS, :], base[0:C:WINDOWS, :])
 
         ones = held.tile([C, C], BF16, name="ones")
-        nc.gpsimd.memset(ones[:], 1.0)
+        nc.vector.memset(ones[:], 1.0)
 
         halves = range(HALVES)
         squares = lent.tile([C, HALVES, H], BF16, name="squares", tag="shared")
@@ -46,4 +46,4 @@ def tile_directionalignmentloss_kernel(tc, base, dirs, offs, out):
 
         for k in range(WINDOWS):
             nc.vector.tensor_tensor(windows[k][:].indirect(offsets[:]), samples[:], scales[:], MULT)
-            nc.sync.dma_start(out[k:C:WINDOWS, :], windows[k][k:C:WINDOWS, :])
+            nc.scalar.dma_start(out[k:C:WINDOWS, :], windows[k][k:C:WINDOWS, :])

import concourse.mybir as mybir

C, S, N = 128, 4096, 512
WINDOWS = 2
HALVES = 2
H = N // HALVES
F32, BF16, U16 = mybir.dt.float32, mybir.dt.bfloat16, mybir.dt.uint16
MULT = mybir.AluOpType.mult
RSQRT = mybir.ActivationFunctionType.Abs_reciprocal_sqrt

FLOPS = 3 * C * N


def tile_directionalignmentloss_kernel(tc, base, dirs, offs, out):
    nc = tc.nc
    with (
        tc.tile_pool(name="held", bufs=1) as held,
        tc.tile_pool(name="lent", bufs=1) as lent,
        tc.psum_pool(name="psum", bufs=1) as psum,
    ):
        samples = held.tile([C, N], F32, name="samples")
        nc.sync.dma_start(samples[:], dirs)
        window0 = held.tile([C, S], F32, name="window0")
        offsets = held.tile([C, N // 16], U16, name="offsets")
        nc.sync.dma_start(offsets[:], offs)
        nc.sync.dma_start(window0[0:C:WINDOWS, :], base[0:C:WINDOWS, :])

        ones = held.tile([C, C], BF16, name="ones")
        nc.vector.memset(ones[:], 1.0)

        halves = range(HALVES)
        squares = lent.tile([C, HALVES, H], BF16, name="squares", tag="shared")
        sums = [psum.tile([C, H], F32, name=f"sums{h}") for h in halves]
        scales = held.tile([C, N], F32, name="scales")

        for h in halves:
            nc.vector.tensor_tensor(squares[:, h, :], samples[:, h * H : (h + 1) * H], samples[:, h * H : (h + 1) * H], MULT)
        for h in halves:
            nc.tensor.matmul(sums[h][:], ones[:], squares[:, h, :], start=True, stop=True)
        for h in halves:
            nc.scalar.activation(scales[:, h * H : (h + 1) * H], sums[h][:], RSQRT)

        window1 = lent.tile([C, S], F32, name="window1", tag="shared")
        nc.sync.dma_start(window1[1:C:WINDOWS, :], base[1:C:WINDOWS, :])
        windows = [window0, window1]

        for k in range(WINDOWS):
            nc.vector.tensor_tensor(windows[k][:].indirect(offsets[:]), samples[:], scales[:], MULT)
            nc.scalar.dma_start(out[k:C:WINDOWS, :], windows[k][k:C:WINDOWS, :])
